import numpy as np
import ml_dtypes


def mxq(x, axis, fmt="e4m3"):
    dtype, down = {"e4m3": (ml_dtypes.float8_e4m3fn, 7), "e5m2": (ml_dtypes.float8_e5m2, 14)}[fmt]
    v = np.moveaxis(np.asarray(x, np.float32).astype(ml_dtypes.bfloat16).astype(np.float64), axis, -1)
    blocks = v.reshape(v.shape[:-1] + (-1, 32))
    amax = np.abs(blocks).max(-1, keepdims=True)
    byte = np.maximum(np.where(amax > 0, np.frexp(amax)[1] - 1 + 127, 0) - down, 1)
    scale = np.exp2(byte - 127.0)
    codes = (blocks / scale).astype(np.float32).astype(dtype).astype(np.float64)
    return np.moveaxis((codes * scale).reshape(v.shape), -1, axis)


WIDE = False


def mx_kscale(k):
    if not WIDE:
        return np.ones(k)
    levels = np.array([10, -10, 5, -5, 0])
    a = np.random.permutation(np.resize(levels, k // 512 * 4)).reshape(k // 512, 4)
    idx = np.arange(k)
    return np.exp2(a[idx // 512, idx % 128 // 32])


BF16 = ml_dtypes.bfloat16


def bf(x):
    return np.asarray(x, np.float32).astype(BF16)


def f64(x):
    return np.asarray(x).astype(np.float64)


B, S, D_MODEL, N_H, D_H, D_CQ, D_CKV, D_HR = 1, 512, 2048, 16, 128, 1024, 512, 128
ROPE_BASE = 10000.0


def rope_cos_sin(seq_len, dim):
    inv_freq = 1.0 / (ROPE_BASE ** (np.arange(0, dim, 2) / dim))
    ang = np.arange(seq_len)[:, None] * inv_freq[None, :]
    return np.cos(ang), np.sin(ang)


def rope(t, cos, sin):
    shp = t.shape
    d2 = shp[-1] // 2
    tr = t.reshape(shp[:-1] + (d2, 2))
    x0, x1 = tr[..., 0], tr[..., 1]
    bshape = (1, shp[1]) + (1,) * (x0.ndim - 3) + (d2,)
    cs, sn = cos.reshape(bshape), sin.reshape(bshape)
    return np.stack([x0 * cs - x1 * sn, x0 * sn + x1 * cs], axis=-1).reshape(shp)


def setup_inputs():
    s, t = mx_kscale(D_MODEL), mx_kscale(D_CKV)
    return {"h": bf(np.random.standard_normal((B, S, D_MODEL)) * s),
            "w_ckv": bf(np.random.standard_normal((D_MODEL, D_CKV)) / np.sqrt(D_MODEL) / s[:, None] * t),
            "w_k": bf(np.random.standard_normal((D_CKV, N_H * D_H)) / np.sqrt(D_CKV) / t[:, None]),
            "w_kr": bf(np.random.standard_normal((D_MODEL, D_HR)) / np.sqrt(D_MODEL) / s[:, None]),
            "w_v": bf(np.random.standard_normal((D_CKV, N_H * D_H)) / np.sqrt(D_CKV) / t[:, None])}


def reference(h, w_ckv, w_k, w_kr, w_v):
    cos, sin = rope_cos_sin(S, D_HR)
    hq = mxq(f64(h), 2, "e4m3")
    c_kv = hq @ mxq(f64(w_ckv), 0, "e4m3")
    cq = mxq(c_kv, 2, "e4m3")
    k_c = (cq @ mxq(f64(w_k), 0, "e4m3")).reshape(B, S, N_H, D_H).transpose(0, 2, 1, 3)
    k_r = rope(hq @ mxq(f64(w_kr), 0, "e4m3"), cos, sin)[:, None]
    k = np.concatenate([k_c, np.broadcast_to(k_r, (B, N_H, S, D_HR))], axis=-1)
    v = (cq @ mxq(f64(w_v), 0, "e4m3")).reshape(B, S, N_H, D_H).transpose(0, 2, 1, 3)
    return k, v

@@ -1,0 +1,237 @@
+import math
+from contextlib import ExitStack
+
+import concourse.mybir as mybir
+from concourse.masks import make_identity
+
+F32 = mybir.dt.float32
+BF16 = mybir.dt.bfloat16
+I32 = mybir.dt.int32
+U32 = mybir.dt.uint32
+U8 = mybir.dt.uint8
+FP8X4 = mybir.dt.float8_e4m3fn_x4
+ALU = mybir.AluOpType
+ACT = mybir.ActivationFunctionType
+
+P = 128
+PACK = 4
+K_PASS = P * PACK
+
+S = 512
+D_MODEL = 2048
+D_CKV = 512
+N_H = 16
+D_H = 128
+D_HR = 128
+PAIRS = D_HR // 2
+PAIR_BITS = 6
+assert 2**PAIR_BITS == PAIRS
+ROPE_BASE = 10000.0
+
+S_TILES = S // P
+PASSES = D_MODEL // K_PASS
+CKV_TILES = D_CKV // P
+GROUP_HEADS = 4
+GROUP_COLS = GROUP_HEADS * D_H
+GROUPS = N_H // GROUP_HEADS
+LOAD_GROUPS = 2
+K_TILES = 2
+ROUND = 1.5 * 2.0**23
+
+FLOPS = 2 * S * (D_MODEL * D_CKV + D_MODEL * D_HR + 2 * D_CKV * N_H * D_H)
+
+
+def tile_mla_pb_kernel(tc, h, w_ckv, w_k, w_kr, w_v, out_0, out_1):
+    nc = tc.nc
+    with ExitStack() as ctx:
+        keep = ctx.enter_context(tc.tile_pool(name="keep", bufs=1))
+        grouped_pool = ctx.enter_context(tc.tile_pool(name="grouped", bufs=3))
+        h_pool = ctx.enter_context(tc.tile_pool(name="h_grouped", bufs=2))
+        banks = ctx.enter_context(tc.psum_pool(name="banks", bufs=7))
+        u_bank = ctx.enter_context(tc.psum_pool(name="u_bank", bufs=1))
+
+        w_ckv_raw = []
+        for g in range(PASSES):
+            raw = keep.tile([P, PACK, D_CKV], BF16, name="w_ckv_raw%d" % g)
+            nc.sync.dma_start(
+                out=raw[:].rearrange("q (u e) c -> q u (e c)", e=2),
+                in_=w_ckv[g * K_PASS : (g + 1) * K_PASS, :].rearrange("(u q e) c -> q u (e c)", u=2, e=2),
+            )
+            w_ckv_raw.append(raw[:])
+        h_rows = h.rearrange("b (p j) k -> p (b j) k", j=S_TILES)
+        h_raw = []
+        for j in range(S_TILES):
+            raw = keep.tile([P, D_MODEL], BF16, name="h_raw%d" % j)
+            nc.sync.dma_start(out=raw[:], in_=h_rows[:, j, :])
+            h_raw.append(raw)
+
+        def load_heads(name, w, part):
+            raw = keep.tile([P, PACK, LOAD_GROUPS * GROUP_COLS], BF16, name="%s_raw%d" % (name, part))
+            first = part * LOAD_GROUPS * GROUP_COLS
+            nc.sync.dma_start(
+                out=raw[:],
+                in_=w.rearrange("(t p) n -> p t n", t=PACK)[:, :, first : first + LOAD_GROUPS * GROUP_COLS],
+            )
+            return [raw[:, :, c * GROUP_COLS : (c + 1) * GROUP_COLS] for c in range(LOAD_GROUPS)]
+
+        w_v_raw = load_heads("w_v", w_v, 0)
+        w_kr_raw = keep.tile([P, PASSES, PACK, D_HR], BF16)
+        nc.sync.dma_start(
+            out=w_kr_raw[:].rearrange("q g (u e) c -> q (g u) (e c)", e=2),
+            in_=w_kr.rearrange("(g u q e) c -> q (g u) (e c)", g=PASSES, u=2, e=2),
+        )
+        w_v_raw = w_v_raw + load_heads("w_v", w_v, 1)
+        w_k_raw = load_heads("w_k", w_k, 0) + load_heads("w_k", w_k, 1)
+
+        identity = keep.tile([P, P], F32)
+        make_identity(nc, identity[:])
+        position = keep.tile([P, S_TILES], I32)
+        nc.gpsimd.iota(position[:], pattern=[[1, S_TILES]], base=0, channel_multiplier=S_TILES)
+        position_turns = keep.tile([P, S_TILES], F32)
+        nc.vector.tensor_scalar_mul(out=position_turns[:], in0=position[:], scalar1=1.0 / (2.0 * math.pi))
+        frequency = keep.tile([P, PAIRS], F32)
+        nc.vector.memset(frequency[:, 0:1], 1.0)
+        for step in range(PAIR_BITS):
+            width = 2**step
+            nc.vector.tensor_scalar_mul(
+                out=frequency[:, width : 2 * width],
+                in0=frequency[:, 0:width],
+                scalar1=ROPE_BASE ** (-2.0 * width / D_HR),
+            )
+        table_shape = [P, S_TILES, PAIRS]
+        phase = keep.tile([P, 2, S_TILES, PAIRS], F32)
+        nc.vector.tensor_mul(
+            out=phase[:, 0],
+            in0=frequency[:].unsqueeze(1).to_broadcast(table_shape),
+            in1=position_turns[:].unsqueeze(2).to_broadcast(table_shape),
+        )
+        nc.vector.tensor_scalar_add(out=phase[:, 1], in0=phase[:, 0], scalar1=0.25)
+        whole = keep.tile([P, 2, S_TILES, PAIRS], F32)
+        nc.vector.tensor_scalar(
+            out=whole[:], in0=phase[:], scalar1=ROUND, scalar2=ROUND, op0=ALU.add, op1=ALU.subtract
+        )
+        part_turn = keep.tile([P, 2, S_TILES, PAIRS], F32)
+        nc.vector.tensor_sub(out=part_turn[:], in0=phase[:], in1=whole[:])
+        sin_cos = keep.tile([P, 2, S_TILES, PAIRS], F32)
+        nc.scalar.activation(out=sin_cos[:], in_=part_turn[:], func=ACT.Sin, scale=2.0 * math.pi)
+
+        def regroup(copy, grouped, raw):
+            copy(
+                out=grouped.rearrange("p (c i) t -> p c t i", i=4),
+                in_=raw.rearrange("p t (c i) -> p c t i", i=4),
+            )
+
+        def quantise(name, grouped_flat):
+            words = grouped_flat.shape[1] // PACK
+            codes = keep.tile([P, words], U32, name=name + "_codes", align_bytes=64)
+            scales = keep.tile([P, words], U8, name=name + "_scales", align_bytes=64)
+            nc.vector.quantize_mx(out=codes[:].bitcast(FP8X4), scales=scales[:], in_=grouped_flat)
+            return codes, scales
+
+        def quantise_weights(name, raws, copies):
+            grouped = []
+            quantised = []
+            for n in range(len(raws) + 1):
+                if n < len(raws):
+                    chunk = grouped_pool.tile([P, GROUP_COLS, PACK], BF16, tag="grouped", align_bytes=64)
+                    regroup(copies[n % len(copies)], chunk[:], raws[n])
+                    grouped.append(chunk)
+                if n > 0:
+                    flat = grouped[n - 1][:].rearrange("p c t -> p (c t)")
+                    quantised.append(quantise("%s%d" % (name, n - 1), flat))
+            return quantised
+
+        def mx(out, stationary, m_cols, moving, n_cols, start, stop):
+            nc.tensor.matmul_mx(
+                out=out,
+                lhsT=stationary[0][:, m_cols].bitcast(FP8X4),
+                lhsT_scale=stationary[1][:, m_cols],
+                rhs=moving[0][:, n_cols].bitcast(FP8X4),
+                rhs_scale=moving[1][:, n_cols],
+                start=start,
+                stop=stop,
+            )
+
+        def block(i):
+            return slice(i * P, (i + 1) * P)
+
+        everything = slice(None)
+
+        w_ckv_q = quantise_weights("w_ckv", w_ckv_raw, [nc.vector.tensor_copy, nc.scalar.copy])
+
+        def transpose_h(j):
+            h_words = h_raw[j][:].bitcast(F32)
+            h_grouped = h_pool.tile([P, D_MODEL], BF16, tag="h_grouped", align_bytes=64)
+            grouped_words = h_grouped[:].bitcast(F32).rearrange("q (g s u) -> q g s u", g=PASSES, u=2)
+            for half in range(2):
+                flipped = banks.tile([P, 2, 2, P], F32, tag="bank")
+                for g in range(2):
+                    for u in range(2):
+                        nc.tensor.transpose(flipped[:, g, u, :], h_words[:, block(4 * half + 2 * g + u)], identity[:])
+                nc.scalar.copy(
+                    out=grouped_words[:, 2 * half : 2 * half + 2], in_=flipped[:].rearrange("q g u s -> q g s u")
+                )
+            return quantise("h%d" % j, h_grouped[:])
+
+        def latent(j):
+            c_kv = banks.tile([P, CKV_TILES, P], F32, tag="bank")
+            for t in range(CKV_TILES):
+                for g in range(PASSES):
+                    mx(c_kv[:, t, :], w_ckv_q[g], block(t), h_q[j], block(g), g == 0, g == PASSES - 1)
+            c_grouped = h_pool.tile([P, P, PACK], BF16, tag="c_grouped", align_bytes=64)
+            nc.scalar.copy(out=c_grouped[:], in_=c_kv[:].rearrange("p t s -> p s t"))
+            return quantise("c_kv%d" % j, c_grouped[:].rearrange("p s t -> p (s t)"))
+
+        h_q = [transpose_h(0)]
+        c_q = []
+        for j in range(S_TILES):
+            if j + 1 < S_TILES:
+                h_q.append(transpose_h(j + 1))
+            c_q.append(latent(j))
+
+        def heads(w_q, out_tile, out_rows):
+            for j in range(S_TILES):
+                product = banks.tile([P, GROUP_HEADS, D_H], F32, tag="bank")
+                mx(product[:].rearrange("p n d -> p (n d)"), c_q[j], everything, w_q, everything, True, True)
+                nc.scalar.copy(out=out_tile[:, :, j, 0:D_H], in_=product[:])
+            nc.sync.dma_start(out=out_rows, in_=out_tile[:].rearrange("p n j d -> p n (j d)"))
+
+        def group(c):
+            return slice(c * GROUP_HEADS, (c + 1) * GROUP_HEADS)
+
+        v_rows = out_1.rearrange("b n (p j) d -> p (b n) (j d)", j=S_TILES)
+        w_v_q = quantise_weights("w_v", w_v_raw, [nc.vector.tensor_copy])
+        for c in range(GROUPS):
+            v_tile = keep.tile([P, GROUP_HEADS, S_TILES, D_H], F32, name="v_tile%d" % c)
+            heads(w_v_q[c], v_tile, v_rows[:, group(c), :])
+
+        kr_grouped = grouped_pool.tile([P, PASSES, D_HR, PACK], BF16, tag="grouped", align_bytes=64)
+        for g in range(PASSES):
+            regroup(nc.vector.tensor_copy, kr_grouped[:, g], w_kr_raw[:, g])
+        w_kr_q = quantise("w_kr", kr_grouped[:].rearrange("p g c t -> p (g c t)"))
+        u_sum = u_bank.tile([P, S_TILES, D_HR], F32)
+        for j in range(S_TILES):
+            for g in range(PASSES):
+                mx(u_sum[:, j, :], h_q[j], block(g), w_kr_q, block(g), g == 0, g == PASSES - 1)
+        u_pairs = u_sum[:].rearrange("p j (i e) -> p e j i", e=2)
+        pair_shape = [P, 2, S_TILES, PAIRS]
+        by_sin = keep.tile(pair_shape, F32)
+        nc.vector.tensor_mul(out=by_sin[:], in0=u_pairs, in1=sin_cos[:, 0].unsqueeze(1).to_broadcast(pair_shape))
+        by_cos = keep.tile(pair_shape, F32)
+        nc.vector.tensor_mul(out=by_cos[:], in0=u_pairs, in1=sin_cos[:, 1].unsqueeze(1).to_broadcast(pair_shape))
+        rotary = keep.tile([P, S_TILES, PAIRS, 2], F32)
+        nc.vector.tensor_sub(out=rotary[:, :, :, 0], in0=by_cos[:, 0], in1=by_sin[:, 1])
+        nc.vector.tensor_add(out=rotary[:, :, :, 1], in0=by_sin[:, 0], in1=by_cos[:, 1])
+        k_tiles = []
+        for i in range(K_TILES):
+            k_tile = keep.tile([P, GROUP_HEADS, S_TILES, D_H + D_HR], F32, name="k_tile%d" % i)
+            nc.vector.tensor_copy(
+                out=k_tile[:, :, :, D_H:],
+                in_=rotary[:].rearrange("p j i e -> p j (i e)").unsqueeze(1).to_broadcast([P, GROUP_HEADS, S_TILES, D_HR]),
+            )
+            k_tiles.append(k_tile)
+
+        k_rows = out_0.rearrange("b n (p j) d -> p (b n) (j d)", j=S_TILES)
+        w_k_q = quantise_weights("w_k", w_k_raw, [nc.vector.tensor_copy])
+        for c in range(GROUPS):
+            heads(w_k_q[c], k_tiles[c % K_TILES], k_rows[:, group(c), :])

@@ -34,7 +34,6 @@ CKV_TILES = D_CKV // P
 GROUP_HEADS = 4
 GROUP_COLS = GROUP_HEADS * D_H
 GROUPS = N_H // GROUP_HEADS
-LOAD_GROUPS = 2
 K_TILES = 2
 ROUND = 1.5 * 2.0**23
 
@@ -45,43 +44,57 @@ def tile_mla_pb_kernel(tc, h, w_ckv, w_k, w_kr, w_v, out_0, out_1):
     nc = tc.nc
     with ExitStack() as ctx:
         keep = ctx.enter_context(tc.tile_pool(name="keep", bufs=1))
-        grouped_pool = ctx.enter_context(tc.tile_pool(name="grouped", bufs=3))
+        grouped_pool = ctx.enter_context(tc.tile_pool(name="grouped", bufs=5))
         h_pool = ctx.enter_context(tc.tile_pool(name="h_grouped", bufs=2))
         banks = ctx.enter_context(tc.psum_pool(name="banks", bufs=7))
         u_bank = ctx.enter_context(tc.psum_pool(name="u_bank", bufs=1))
+        ctx.enter_context(tc.manual_schedule())
+
+        def block(i):
+            return slice(i * P, (i + 1) * P)
+
+        everything = slice(None)
+
+        h_rows = h.rearrange("b (p j) k -> p (b j) k", j=S_TILES)
+        h_raw = []
+
+        def load_h(j):
+            raw = keep.tile([P, D_MODEL], BF16, name="h_raw%d" % j)
+            nc.sync.dma_start(out=raw[:], in_=h_rows[:, j, :])
+            h_raw.append(raw)
 
         w_ckv_raw = []
-        for g in range(PASSES):
+
+        def load_w_ckv(g):
             raw = keep.tile([P, PACK, D_CKV], BF16, name="w_ckv_raw%d" % g)
             nc.sync.dma_start(
                 out=raw[:].rearrange("q (u e) c -> q u (e c)", e=2),
                 in_=w_ckv[g * K_PASS : (g + 1) * K_PASS, :].rearrange("(u q e) c -> q u (e c)", u=2, e=2),
             )
             w_ckv_raw.append(raw[:])
-        h_rows = h.rearrange("b (p j) k -> p (b j) k", j=S_TILES)
-        h_raw = []
-        for j in range(S_TILES):
-            raw = keep.tile([P, D_MODEL], BF16, name="h_raw%d" % j)
-            nc.sync.dma_start(out=raw[:], in_=h_rows[:, j, :])
-            h_raw.append(raw)
 
-        def load_heads(name, w, part):
-            raw = keep.tile([P, PACK, LOAD_GROUPS * GROUP_COLS], BF16, name="%s_raw%d" % (name, part))
-            first = part * LOAD_GROUPS * GROUP_COLS
+        def load_heads(name, w, first_group, groups):
+            raw = keep.tile([P, PACK, groups * GROUP_COLS], BF16, name="%s_raw%d" % (name, first_group))
+            first = first_group * GROUP_COLS
             nc.sync.dma_start(
                 out=raw[:],
-                in_=w.rearrange("(t p) n -> p t n", t=PACK)[:, :, first : first + LOAD_GROUPS * GROUP_COLS],
+                in_=w.rearrange("(t p) n -> p t n", t=PACK)[:, :, first : first + groups * GROUP_COLS],
             )
-            return [raw[:, :, c * GROUP_COLS : (c + 1) * GROUP_COLS] for c in range(LOAD_GROUPS)]
+            return [raw[:, :, c * GROUP_COLS : (c + 1) * GROUP_COLS] for c in range(groups)]
 
-        w_v_raw = load_heads("w_v", w_v, 0)
+        load_h(0)
+        for g in range(PASSES):
+            load_w_ckv(g)
+        load_h(1)
         w_kr_raw = keep.tile([P, PASSES, PACK, D_HR], BF16)
         nc.sync.dma_start(
             out=w_kr_raw[:].rearrange("q g (u e) c -> q (g u) (e c)", e=2),
             in_=w_kr.rearrange("(g u q e) c -> q (g u) (e c)", g=PASSES, u=2, e=2),
         )
-        w_v_raw = w_v_raw + load_heads("w_v", w_v, 1)
-        w_k_raw = load_heads("w_k", w_k, 0) + load_heads("w_k", w_k, 1)
+        load_h(2)
+        load_h(3)
+        w_v_raw = load_heads("w_v", w_v, 0, 2) + load_heads("w_v", w_v, 2, 2)
+        w_k_raw = load_heads("w_k", w_k, 0, GROUPS)
 
         identity = keep.tile([P, P], F32)
         make_identity(nc, identity[:])
@@ -112,14 +125,25 @@ def tile_mla_pb_kernel(tc, h, w_ckv, w_k, w_kr, w_v, out_0, out_1):
         )
         part_turn = keep.tile([P, 2, S_TILES, PAIRS], F32)
         nc.vector.tensor_sub(out=part_turn[:], in0=phase[:], in1=whole[:])
-        sin_cos = keep.tile([P, 2, S_TILES, PAIRS], F32)
-        nc.scalar.activation(out=sin_cos[:], in_=part_turn[:], func=ACT.Sin, scale=2.0 * math.pi)
+        signed_sin = keep.tile([P, S_TILES, PAIRS, 2], F32)
+        nc.scalar.activation(out=signed_sin[:, :, :, 0], in_=part_turn[:, 0], func=ACT.Sin, scale=-2.0 * math.pi)
+        nc.scalar.activation(out=signed_sin[:, :, :, 1], in_=part_turn[:, 0], func=ACT.Sin, scale=2.0 * math.pi)
+        cosine = keep.tile([P, S_TILES, PAIRS], F32)
+        nc.scalar.activation(out=cosine[:], in_=part_turn[:, 1], func=ACT.Sin, scale=2.0 * math.pi)
 
         def regroup(copy, grouped, raw):
             copy(
                 out=grouped.rearrange("p (c i) t -> p c t i", i=4),
                 in_=raw.rearrange("p t (c i) -> p c t i", i=4),
             )
+
+        def new_chunk():
+            return grouped_pool.tile([P, GROUP_COLS, PACK], BF16, tag="grouped", name="chunk", align_bytes=64)
+
+        def regrouped(copy, raw):
+            chunk = new_chunk()
+            regroup(copy, chunk[:], raw)
+            return chunk
 
         def quantise(name, grouped_flat):
             words = grouped_flat.shape[1] // PACK
@@ -128,18 +152,8 @@ def tile_mla_pb_kernel(tc, h, w_ckv, w_k, w_kr, w_v, out_0, out_1):
             nc.vector.quantize_mx(out=codes[:].bitcast(FP8X4), scales=scales[:], in_=grouped_flat)
             return codes, scales
 
-        def quantise_weights(name, raws, copies):
-            grouped = []
-            quantised = []
-            for n in range(len(raws) + 1):
-                if n < len(raws):
-                    chunk = grouped_pool.tile([P, GROUP_COLS, PACK], BF16, tag="grouped", align_bytes=64)
-                    regroup(copies[n % len(copies)], chunk[:], raws[n])
-                    grouped.append(chunk)
-                if n > 0:
-                    flat = grouped[n - 1][:].rearrange("p c t -> p (c t)")
-                    quantised.append(quantise("%s%d" % (name, n - 1), flat))
-            return quantised
+        def quantise_chunk(name, chunk):
+            return quantise(name, chunk[:].rearrange("p c t -> p (c t)"))
 
         def mx(out, stationary, m_cols, moving, n_cols, start, stop):
             nc.tensor.matmul_mx(
@@ -151,13 +165,6 @@ def tile_mla_pb_kernel(tc, h, w_ckv, w_k, w_kr, w_v, out_0, out_1):
                 start=start,
                 stop=stop,
             )
-
-        def block(i):
-            return slice(i * P, (i + 1) * P)
-
-        everything = slice(None)
-
-        w_ckv_q = quantise_weights("w_ckv", w_ckv_raw, [nc.vector.tensor_copy, nc.scalar.copy])
 
         def transpose_h(j):
             h_words = h_raw[j][:].bitcast(F32)
@@ -171,7 +178,12 @@ def tile_mla_pb_kernel(tc, h, w_ckv, w_k, w_kr, w_v, out_0, out_1):
                 nc.scalar.copy(
                     out=grouped_words[:, 2 * half : 2 * half + 2], in_=flipped[:].rearrange("q g u s -> q g s u")
                 )
-            return quantise("h%d" % j, h_grouped[:])
+            return h_grouped
+
+        h_q = []
+
+        def quantise_h(h_grouped):
+            h_q.append(quantise("h%d" % len(h_q), h_grouped[:]))
 
         def latent(j):
             c_kv = banks.tile([P, CKV_TILES, P], F32, tag="bank")
@@ -180,58 +192,125 @@ def tile_mla_pb_kernel(tc, h, w_ckv, w_k, w_kr, w_v, out_0, out_1):
                     mx(c_kv[:, t, :], w_ckv_q[g], block(t), h_q[j], block(g), g == 0, g == PASSES - 1)
             c_grouped = h_pool.tile([P, P, PACK], BF16, tag="c_grouped", align_bytes=64)
             nc.scalar.copy(out=c_grouped[:], in_=c_kv[:].rearrange("p t s -> p s t"))
-            return quantise("c_kv%d" % j, c_grouped[:].rearrange("p s t -> p (s t)"))
+            return c_grouped
 
-        h_q = [transpose_h(0)]
         c_q = []
-        for j in range(S_TILES):
-            if j + 1 < S_TILES:
-                h_q.append(transpose_h(j + 1))
-            c_q.append(latent(j))
 
-        def heads(w_q, out_tile, out_rows):
-            for j in range(S_TILES):
-                product = banks.tile([P, GROUP_HEADS, D_H], F32, tag="bank")
-                mx(product[:].rearrange("p n d -> p (n d)"), c_q[j], everything, w_q, everything, True, True)
-                nc.scalar.copy(out=out_tile[:, :, j, 0:D_H], in_=product[:])
+        def quantise_c(c_grouped):
+            c_q.append(quantise("c_kv%d" % len(c_q), c_grouped[:].rearrange("p s t -> p (s t)")))
+
+        def product(j, w_q, out_tile, copy):
+            bank = banks.tile([P, GROUP_HEADS, D_H], F32, tag="bank")
+            mx(bank[:].rearrange("p n d -> p (n d)"), c_q[j], everything, w_q, everything, True, True)
+            copy(out=out_tile[:, :, j, 0:D_H], in_=bank[:])
+
+        def store(out_tile, out_rows):
             nc.sync.dma_start(out=out_rows, in_=out_tile[:].rearrange("p n j d -> p n (j d)"))
 
         def group(c):
             return slice(c * GROUP_HEADS, (c + 1) * GROUP_HEADS)
 
-        v_rows = out_1.rearrange("b n (p j) d -> p (b n) (j d)", j=S_TILES)
-        w_v_q = quantise_weights("w_v", w_v_raw, [nc.vector.tensor_copy])
-        for c in range(GROUPS):
-            v_tile = keep.tile([P, GROUP_HEADS, S_TILES, D_H], F32, name="v_tile%d" % c)
-            heads(w_v_q[c], v_tile, v_rows[:, group(c), :])
+        on_vector = nc.vector.tensor_copy
+        on_scalar = nc.scalar.copy
+
+        def half_regroup(copy, chunk, raw, half):
+            cols = slice(half * GROUP_COLS // 2, (half + 1) * GROUP_COLS // 2)
+            regroup(copy, chunk[:, cols], raw[:, :, cols])
 
         kr_grouped = grouped_pool.tile([P, PASSES, D_HR, PACK], BF16, tag="grouped", align_bytes=64)
-        for g in range(PASSES):
-            regroup(nc.vector.tensor_copy, kr_grouped[:, g], w_kr_raw[:, g])
+
+        def half_regroup_kr(half):
+            passes = slice(half * PASSES // 2, (half + 1) * PASSES // 2)
+            nc.scalar.copy(out=kr_grouped[:, passes], in_=w_kr_raw[:, passes].rearrange("p g t c -> p g c t"))
+
+        h_g0 = transpose_h(0)
+        w0 = regrouped(on_vector, w_ckv_raw[0])
+        quantise_h(h_g0)
+        w1 = regrouped(on_scalar, w_ckv_raw[1])
+        w_ckv_q = [quantise_chunk("w_ckv0", w0)]
+        w2 = regrouped(on_vector, w_ckv_raw[2])
+        w3 = new_chunk()
+        half_regroup(on_vector, w3, w_ckv_raw[3], 0)
+        half_regroup(on_scalar, w3, w_ckv_raw[3], 1)
+        h_g1 = transpose_h(1)
+        w_ckv_q.append(quantise_chunk("w_ckv1", w1))
+        w_ckv_q.append(quantise_chunk("w_ckv2", w2))
+        w_ckv_q.append(quantise_chunk("w_ckv3", w3))
+        half_regroup_kr(0)
+        quantise_h(h_g1)
+        c_g0 = latent(0)
+        h_g2 = transpose_h(2)
+        quantise_c(c_g0)
+        quantise_h(h_g2)
+        c_g1 = latent(1)
+        h_g3 = transpose_h(3)
+        quantise_c(c_g1)
+        v0 = new_chunk()
+        half_regroup(on_vector, v0, w_v_raw[0], 0)
+        quantise_h(h_g3)
+        c_g2 = latent(2)
+        half_regroup(on_vector, v0, w_v_raw[0], 1)
+        half_regroup_kr(1)
+        c_g3 = latent(3)
+        quantise_c(c_g2)
+        v_q = [quantise_chunk("w_v0", v0)]
+        v1 = new_chunk()
+        half_regroup(on_vector, v1, w_v_raw[1], 0)
+        quantise_c(c_g3)
+        half_regroup(on_vector, v1, w_v_raw[1], 1)
+
+        v_rows = out_1.rearrange("b n (p j) d -> p (b n) (j d)", j=S_TILES)
+        k_rows = out_0.rearrange("b n (p j) d -> p (b n) (j d)", j=S_TILES)
+
+        def heads(w_q, out_tile, out_rows, copies):
+            for j in range(S_TILES):
+                product(j, w_q, out_tile, copies[j % len(copies)])
+            store(out_tile, out_rows)
+
+        def new_v_tile(c):
+            return keep.tile([P, GROUP_HEADS, S_TILES, D_H], F32, name="v_tile%d" % c)
+
+        heads(v_q[0], new_v_tile(0), v_rows[:, group(0), :], [on_scalar])
+        v_q.append(quantise_chunk("w_v1", v1))
         w_kr_q = quantise("w_kr", kr_grouped[:].rearrange("p g c t -> p (g c t)"))
+        heads(v_q[1], new_v_tile(1), v_rows[:, group(1), :], [on_scalar])
         u_sum = u_bank.tile([P, S_TILES, D_HR], F32)
         for j in range(S_TILES):
             for g in range(PASSES):
                 mx(u_sum[:, j, :], h_q[j], block(g), w_kr_q, block(g), g == 0, g == PASSES - 1)
-        u_pairs = u_sum[:].rearrange("p j (i e) -> p e j i", e=2)
-        pair_shape = [P, 2, S_TILES, PAIRS]
-        by_sin = keep.tile(pair_shape, F32)
-        nc.vector.tensor_mul(out=by_sin[:], in0=u_pairs, in1=sin_cos[:, 0].unsqueeze(1).to_broadcast(pair_shape))
+        v2 = regrouped(on_vector, w_v_raw[2])
+        v_q.append(quantise_chunk("w_v2", v2))
+        heads(v_q[2], new_v_tile(2), v_rows[:, group(2), :], [on_scalar])
+
+        pair_shape = [P, S_TILES, PAIRS, 2]
+        u_pairs = u_sum[:].rearrange("p j (i e) -> p j i e", e=2)
+        v3 = regrouped(on_vector, w_v_raw[3])
         by_cos = keep.tile(pair_shape, F32)
-        nc.vector.tensor_mul(out=by_cos[:], in0=u_pairs, in1=sin_cos[:, 1].unsqueeze(1).to_broadcast(pair_shape))
-        rotary = keep.tile([P, S_TILES, PAIRS, 2], F32)
-        nc.vector.tensor_sub(out=rotary[:, :, :, 0], in0=by_cos[:, 0], in1=by_sin[:, 1])
-        nc.vector.tensor_add(out=rotary[:, :, :, 1], in0=by_sin[:, 0], in1=by_cos[:, 1])
+        nc.vector.tensor_mul(out=by_cos[:], in0=u_pairs, in1=cosine[:].unsqueeze(3).to_broadcast(pair_shape))
+        v_q.append(quantise_chunk("w_v3", v3))
+        heads(v_q[3], new_v_tile(3), v_rows[:, group(3), :], [on_scalar])
+        by_sin = keep.tile(pair_shape, F32)
+        nc.vector.tensor_mul(out=by_sin[:], in0=u_pairs[:, :, :, ::-1], in1=signed_sin[:])
+        k_chunk = new_chunk()
+        half_regroup(on_vector, k_chunk, w_k_raw[0], 0)
+        rotary = keep.tile([P, S_TILES, D_HR], F32)
+        nc.vector.tensor_add(out=rotary[:].rearrange("p j (i e) -> p j i e", e=2), in0=by_cos[:], in1=by_sin[:])
+        half_regroup(on_vector, k_chunk, w_k_raw[0], 1)
+
         k_tiles = []
-        for i in range(K_TILES):
-            k_tile = keep.tile([P, GROUP_HEADS, S_TILES, D_H + D_HR], F32, name="k_tile%d" % i)
-            nc.vector.tensor_copy(
-                out=k_tile[:, :, :, D_H:],
-                in_=rotary[:].rearrange("p j i e -> p j (i e)").unsqueeze(1).to_broadcast([P, GROUP_HEADS, S_TILES, D_HR]),
-            )
+
+        def new_k_tile():
+            k_tile = keep.tile([P, GROUP_HEADS, S_TILES, D_H + D_HR], F32, name="k_tile%d" % len(k_tiles))
+            half = GROUP_HEADS // 2
+            source = rotary[:].unsqueeze(1).to_broadcast([P, half, S_TILES, D_HR])
+            nc.vector.tensor_copy(out=k_tile[:, 0:half, :, D_H:], in_=source)
+            nc.scalar.copy(out=k_tile[:, half:, :, D_H:], in_=source)
             k_tiles.append(k_tile)
 
-        k_rows = out_0.rearrange("b n (p j) d -> p (b n) (j d)", j=S_TILES)
-        w_k_q = quantise_weights("w_k", w_k_raw, [nc.vector.tensor_copy])
         for c in range(GROUPS):
-            heads(w_k_q[c], k_tiles[c % K_TILES], k_rows[:, group(c), :])
+            if c < K_TILES:
+                new_k_tile()
+            k_q = quantise_chunk("w_k%d" % c, k_chunk)
+            heads(k_q, k_tiles[c % K_TILES], k_rows[:, group(c), :], [on_scalar, on_vector])
+            if c + 1 < GROUPS:
+                k_chunk = regrouped(on_vector, w_k_raw[c + 1])

@@ -34,7 +34,7 @@ CKV_TILES = D_CKV // P
 GROUP_HEADS = 4
 GROUP_COLS = GROUP_HEADS * D_H
 GROUPS = N_H // GROUP_HEADS
-K_TILES = 2
+K_TILES = 3
 ROUND = 1.5 * 2.0**23
 
 FLOPS = 2 * S * (D_MODEL * D_CKV + D_MODEL * D_HR + 2 * D_CKV * N_H * D_H)
@@ -44,8 +44,9 @@ def tile_mla_pb_kernel(tc, h, w_ckv, w_k, w_kr, w_v, out_0, out_1):
     nc = tc.nc
     with ExitStack() as ctx:
         keep = ctx.enter_context(tc.tile_pool(name="keep", bufs=1))
-        grouped_pool = ctx.enter_context(tc.tile_pool(name="grouped", bufs=5))
-        h_pool = ctx.enter_context(tc.tile_pool(name="h_grouped", bufs=2))
+        grouped_pool = ctx.enter_context(tc.tile_pool(name="grouped", bufs=4))
+        h_pool = ctx.enter_context(tc.tile_pool(name="h_grouped", bufs=3))
+        v_pool = ctx.enter_context(tc.tile_pool(name="v_tiles", bufs=3))
         banks = ctx.enter_context(tc.psum_pool(name="banks", bufs=7))
         u_bank = ctx.enter_context(tc.psum_pool(name="u_bank", bufs=1))
         ctx.enter_context(tc.manual_schedule())
@@ -100,6 +101,9 @@ def tile_mla_pb_kernel(tc, h, w_ckv, w_k, w_kr, w_v, out_0, out_1):
         make_identity(nc, identity[:])
         position = keep.tile([P, S_TILES], I32)
         nc.gpsimd.iota(position[:], pattern=[[1, S_TILES]], base=0, channel_multiplier=S_TILES)
+        first_sine = keep.tile([P, 1], F32)
+        nc.vector.memset(first_sine[:], 0.0)
+        nc.scalar.activation(out=first_sine[:], in_=first_sine[:], func=ACT.Sin)
         position_turns = keep.tile([P, S_TILES], F32)
         nc.vector.tensor_scalar_mul(out=position_turns[:], in0=position[:], scalar1=1.0 / (2.0 * math.pi))
         frequency = keep.tile([P, PAIRS], F32)
@@ -120,16 +124,25 @@ def tile_mla_pb_kernel(tc, h, w_ckv, w_k, w_kr, w_v, out_0, out_1):
         )
         nc.vector.tensor_scalar_add(out=phase[:, 1], in0=phase[:, 0], scalar1=0.25)
         whole = keep.tile([P, 2, S_TILES, PAIRS], F32)
-        nc.vector.tensor_scalar(
-            out=whole[:], in0=phase[:], scalar1=ROUND, scalar2=ROUND, op0=ALU.add, op1=ALU.subtract
-        )
         part_turn = keep.tile([P, 2, S_TILES, PAIRS], F32)
-        nc.vector.tensor_sub(out=part_turn[:], in0=phase[:], in1=whole[:])
         signed_sin = keep.tile([P, S_TILES, PAIRS, 2], F32)
-        nc.scalar.activation(out=signed_sin[:, :, :, 0], in_=part_turn[:, 0], func=ACT.Sin, scale=-2.0 * math.pi)
-        nc.scalar.activation(out=signed_sin[:, :, :, 1], in_=part_turn[:, 0], func=ACT.Sin, scale=2.0 * math.pi)
         cosine = keep.tile([P, S_TILES, PAIRS], F32)
-        nc.scalar.activation(out=cosine[:], in_=part_turn[:, 1], func=ACT.Sin, scale=2.0 * math.pi)
+
+        def round_turns():
+            nc.vector.tensor_scalar(
+                out=whole[:], in0=phase[:], scalar1=ROUND, scalar2=ROUND, op0=ALU.add, op1=ALU.subtract
+            )
+
+        def part_turns():
+            nc.vector.tensor_sub(out=part_turn[:], in0=phase[:], in1=whole[:])
+
+        def sines():
+            for e in range(2):
+                scale = (2 * e - 1) * 2.0 * math.pi
+                nc.scalar.activation(out=signed_sin[:, :, :, e], in_=part_turn[:, 0], func=ACT.Sin, scale=scale)
+
+        def cosines():
+            nc.scalar.activation(out=cosine[:], in_=part_turn[:, 1], func=ACT.Sin, scale=2.0 * math.pi)
 
         def regroup(copy, grouped, raw):
             copy(
@@ -180,18 +193,23 @@ def tile_mla_pb_kernel(tc, h, w_ckv, w_k, w_kr, w_v, out_0, out_1):
                 )
             return h_grouped
 
+        def warm(g):
+            bank = u_bank.tile([P, D_CKV], F32, tag="u")
+            for t in range(2):
+                nc.tensor.matmul(bank[:], w_ckv_raw[g][:, t, 0:P], w_ckv_raw[g][:, t + 2, :], start=True, stop=True)
+
         h_q = []
 
         def quantise_h(h_grouped):
             h_q.append(quantise("h%d" % len(h_q), h_grouped[:]))
 
-        def latent(j):
+        def latent(j, copy):
             c_kv = banks.tile([P, CKV_TILES, P], F32, tag="bank")
             for t in range(CKV_TILES):
                 for g in range(PASSES):
                     mx(c_kv[:, t, :], w_ckv_q[g], block(t), h_q[j], block(g), g == 0, g == PASSES - 1)
             c_grouped = h_pool.tile([P, P, PACK], BF16, tag="c_grouped", align_bytes=64)
-            nc.scalar.copy(out=c_grouped[:], in_=c_kv[:].rearrange("p t s -> p s t"))
+            copy(out=c_grouped[:], in_=c_kv[:].rearrange("p t s -> p s t"))
             return c_grouped
 
         c_q = []
@@ -217,13 +235,15 @@ def tile_mla_pb_kernel(tc, h, w_ckv, w_k, w_kr, w_v, out_0, out_1):
             cols = slice(half * GROUP_COLS // 2, (half + 1) * GROUP_COLS // 2)
             regroup(copy, chunk[:, cols], raw[:, :, cols])
 
-        kr_grouped = grouped_pool.tile([P, PASSES, D_HR, PACK], BF16, tag="grouped", align_bytes=64)
+        kr_grouped = keep.tile([P, PASSES, D_HR, PACK], BF16, align_bytes=64)
 
         def half_regroup_kr(half):
             passes = slice(half * PASSES // 2, (half + 1) * PASSES // 2)
             nc.scalar.copy(out=kr_grouped[:, passes], in_=w_kr_raw[:, passes].rearrange("p g t c -> p g c t"))
 
         h_g0 = transpose_h(0)
+        for g in range(PASSES):
+            warm(g)
         w0 = regrouped(on_vector, w_ckv_raw[0])
         quantise_h(h_g0)
         w1 = regrouped(on_scalar, w_ckv_raw[1])
@@ -238,26 +258,26 @@ def tile_mla_pb_kernel(tc, h, w_ckv, w_k, w_kr, w_v, out_0, out_1):
         w_ckv_q.append(quantise_chunk("w_ckv3", w3))
         half_regroup_kr(0)
         quantise_h(h_g1)
-        c_g0 = latent(0)
+        round_turns()
+        c_g0 = latent(0, on_scalar)
         h_g2 = transpose_h(2)
-        quantise_c(c_g0)
-        quantise_h(h_g2)
-        c_g1 = latent(1)
+        warm(0)
         h_g3 = transpose_h(3)
-        quantise_c(c_g1)
-        v0 = new_chunk()
-        half_regroup(on_vector, v0, w_v_raw[0], 0)
-        quantise_h(h_g3)
-        c_g2 = latent(2)
-        half_regroup(on_vector, v0, w_v_raw[0], 1)
+        quantise_c(c_g0)
+        part_turns()
+        quantise_h(h_g2)
         half_regroup_kr(1)
-        c_g3 = latent(3)
-        quantise_c(c_g2)
+        quantise_h(h_g3)
+        c_g1 = latent(1, on_scalar)
+        v0 = regrouped(on_vector, w_v_raw[0])
+        c_g2 = latent(2, on_scalar)
+        quantise_c(c_g1)
         v_q = [quantise_chunk("w_v0", v0)]
-        v1 = new_chunk()
-        half_regroup(on_vector, v1, w_v_raw[1], 0)
+        sines()
+        c_g3 = latent(3, on_scalar)
+        quantise_c(c_g2)
+        v1 = regrouped(on_vector, w_v_raw[1])
         quantise_c(c_g3)
-        half_regroup(on_vector, v1, w_v_raw[1], 1)
 
         v_rows = out_1.rearrange("b n (p j) d -> p (b n) (j d)", j=S_TILES)
         k_rows = out_0.rearrange("b n (p j) d -> p (b n) (j d)", j=S_TILES)
@@ -268,23 +288,26 @@ def tile_mla_pb_kernel(tc, h, w_ckv, w_k, w_kr, w_v, out_0, out_1):
             store(out_tile, out_rows)
 
         def new_v_tile(c):
-            return keep.tile([P, GROUP_HEADS, S_TILES, D_H], F32, name="v_tile%d" % c)
+            return v_pool.tile([P, GROUP_HEADS, S_TILES, D_H], F32, tag="v_tile", name="v_tile%d" % c)
 
         heads(v_q[0], new_v_tile(0), v_rows[:, group(0), :], [on_scalar])
         v_q.append(quantise_chunk("w_v1", v1))
         w_kr_q = quantise("w_kr", kr_grouped[:].rearrange("p g c t -> p (g c t)"))
         heads(v_q[1], new_v_tile(1), v_rows[:, group(1), :], [on_scalar])
-        u_sum = u_bank.tile([P, S_TILES, D_HR], F32)
+        cosines()
+        u_sum = u_bank.tile([P, S_TILES, D_HR], F32, tag="u")
         for j in range(S_TILES):
             for g in range(PASSES):
                 mx(u_sum[:, j, :], h_q[j], block(g), w_kr_q, block(g), g == 0, g == PASSES - 1)
         v2 = regrouped(on_vector, w_v_raw[2])
+        v3 = new_chunk()
+        half_regroup(on_vector, v3, w_v_raw[3], 0)
         v_q.append(quantise_chunk("w_v2", v2))
         heads(v_q[2], new_v_tile(2), v_rows[:, group(2), :], [on_scalar])
 
         pair_shape = [P, S_TILES, PAIRS, 2]
         u_pairs = u_sum[:].rearrange("p j (i e) -> p j i e", e=2)
-        v3 = regrouped(on_vector, w_v_raw[3])
+        half_regroup(on_vector, v3, w_v_raw[3], 1)
         by_cos = keep.tile(pair_shape, F32)
         nc.vector.tensor_mul(out=by_cos[:], in0=u_pairs, in1=cosine[:].unsqueeze(3).to_broadcast(pair_shape))
         v_q.append(quantise_chunk("w_v3", v3))
@@ -307,10 +330,13 @@ def tile_mla_pb_kernel(tc, h, w_ckv, w_k, w_kr, w_v, out_0, out_1):
             nc.scalar.copy(out=k_tile[:, half:, :, D_H:], in_=source)
             k_tiles.append(k_tile)
 
+        new_k_tile()
+        k_q = quantise_chunk("w_k0", k_chunk)
         for c in range(GROUPS):
-            if c < K_TILES:
-                new_k_tile()
-            k_q = quantise_chunk("w_k%d" % c, k_chunk)
-            heads(k_q, k_tiles[c % K_TILES], k_rows[:, group(c), :], [on_scalar, on_vector])
             if c + 1 < GROUPS:
                 k_chunk = regrouped(on_vector, w_k_raw[c + 1])
+            heads(k_q, k_tiles[c % K_TILES], k_rows[:, group(c), :], [on_scalar, on_vector])
+            if c + 1 < K_TILES:
+                new_k_tile()
+            if c + 1 < GROUPS:
+                k_q = quantise_chunk("w_k%d" % (c + 1), k_chunk)

@@ -87,14 +87,15 @@ def tile_mla_pb_kernel(tc, h, w_ckv, w_k, w_kr, w_v, out_0, out_1):
         for g in range(PASSES):
             load_w_ckv(g)
         load_h(1)
+        load_h(2)
+        load_h(3)
+        w_v_raw = load_heads("w_v", w_v, 0, 2)
         w_kr_raw = keep.tile([P, PASSES, PACK, D_HR], BF16)
         nc.sync.dma_start(
             out=w_kr_raw[:].rearrange("q g (u e) c -> q (g u) (e c)", e=2),
             in_=w_kr.rearrange("(g u q e) c -> q (g u) (e c)", g=PASSES, u=2, e=2),
         )
-        load_h(2)
-        load_h(3)
-        w_v_raw = load_heads("w_v", w_v, 0, 2) + load_heads("w_v", w_v, 2, 2)
+        w_v_raw = w_v_raw + load_heads("w_v", w_v, 2, 2)
         w_k_raw = load_heads("w_k", w_k, 0, GROUPS)
 
         identity = keep.tile([P, P], F32)
@@ -235,12 +236,6 @@ def tile_mla_pb_kernel(tc, h, w_ckv, w_k, w_kr, w_v, out_0, out_1):
             cols = slice(half * GROUP_COLS // 2, (half + 1) * GROUP_COLS // 2)
             regroup(copy, chunk[:, cols], raw[:, :, cols])
 
-        kr_grouped = keep.tile([P, PASSES, D_HR, PACK], BF16, align_bytes=64)
-
-        def half_regroup_kr(half):
-            passes = slice(half * PASSES // 2, (half + 1) * PASSES // 2)
-            nc.scalar.copy(out=kr_grouped[:, passes], in_=w_kr_raw[:, passes].rearrange("p g t c -> p g c t"))
-
         h_g0 = transpose_h(0)
         for g in range(PASSES):
             warm(g)
@@ -256,24 +251,25 @@ def tile_mla_pb_kernel(tc, h, w_ckv, w_k, w_kr, w_v, out_0, out_1):
         w_ckv_q.append(quantise_chunk("w_ckv1", w1))
         w_ckv_q.append(quantise_chunk("w_ckv2", w2))
         w_ckv_q.append(quantise_chunk("w_ckv3", w3))
-        half_regroup_kr(0)
+        h_g2 = transpose_h(2)
+        warm(0)
         quantise_h(h_g1)
         round_turns()
         c_g0 = latent(0, on_scalar)
-        h_g2 = transpose_h(2)
-        warm(0)
         h_g3 = transpose_h(3)
-        quantise_c(c_g0)
-        part_turns()
         quantise_h(h_g2)
-        half_regroup_kr(1)
-        quantise_h(h_g3)
+        part_turns()
+        quantise_c(c_g0)
         c_g1 = latent(1, on_scalar)
-        v0 = regrouped(on_vector, w_v_raw[0])
+        sines()
+        cosines()
+        v0 = new_chunk()
+        half_regroup(on_vector, v0, w_v_raw[0], 0)
+        quantise_h(h_g3)
+        half_regroup(on_vector, v0, w_v_raw[0], 1)
         c_g2 = latent(2, on_scalar)
         quantise_c(c_g1)
         v_q = [quantise_chunk("w_v0", v0)]
-        sines()
         c_g3 = latent(3, on_scalar)
         quantise_c(c_g2)
         v1 = regrouped(on_vector, w_v_raw[1])
@@ -292,51 +288,63 @@ def tile_mla_pb_kernel(tc, h, w_ckv, w_k, w_kr, w_v, out_0, out_1):
 
         heads(v_q[0], new_v_tile(0), v_rows[:, group(0), :], [on_scalar])
         v_q.append(quantise_chunk("w_v1", v1))
-        w_kr_q = quantise("w_kr", kr_grouped[:].rearrange("p g c t -> p (g c t)"))
         heads(v_q[1], new_v_tile(1), v_rows[:, group(1), :], [on_scalar])
-        cosines()
+
+        kr_grouped = keep.tile([P, PASSES, D_HR, PACK], BF16, align_bytes=64)
+
+        def half_regroup_kr(half):
+            passes = slice(half * PASSES // 2, (half + 1) * PASSES // 2)
+            nc.vector.tensor_copy(out=kr_grouped[:, passes], in_=w_kr_raw[:, passes].rearrange("p g t c -> p g c t"))
+
+        v2 = regrouped(on_vector, w_v_raw[2])
+        half_regroup_kr(0)
+        v_q.append(quantise_chunk("w_v2", v2))
+        heads(v_q[2], new_v_tile(2), v_rows[:, group(2), :], [on_scalar])
+        v3 = regrouped(on_vector, w_v_raw[3])
+        half_regroup_kr(1)
+        v_q.append(quantise_chunk("w_v3", v3))
+        w_kr_q = quantise("w_kr", kr_grouped[:].rearrange("p g c t -> p (g c t)"))
+        heads(v_q[3], new_v_tile(3), v_rows[:, group(3), :], [on_scalar])
         u_sum = u_bank.tile([P, S_TILES, D_HR], F32, tag="u")
         for j in range(S_TILES):
             for g in range(PASSES):
                 mx(u_sum[:, j, :], h_q[j], block(g), w_kr_q, block(g), g == 0, g == PASSES - 1)
-        v2 = regrouped(on_vector, w_v_raw[2])
-        v3 = new_chunk()
-        half_regroup(on_vector, v3, w_v_raw[3], 0)
-        v_q.append(quantise_chunk("w_v2", v2))
-        heads(v_q[2], new_v_tile(2), v_rows[:, group(2), :], [on_scalar])
 
         pair_shape = [P, S_TILES, PAIRS, 2]
         u_pairs = u_sum[:].rearrange("p j (i e) -> p j i e", e=2)
-        half_regroup(on_vector, v3, w_v_raw[3], 1)
+        k_chunk = regrouped(on_vector, w_k_raw[0])
+        k_q = quantise_chunk("w_k0", k_chunk)
         by_cos = keep.tile(pair_shape, F32)
         nc.vector.tensor_mul(out=by_cos[:], in0=u_pairs, in1=cosine[:].unsqueeze(3).to_broadcast(pair_shape))
-        v_q.append(quantise_chunk("w_v3", v3))
-        heads(v_q[3], new_v_tile(3), v_rows[:, group(3), :], [on_scalar])
         by_sin = keep.tile(pair_shape, F32)
         nc.vector.tensor_mul(out=by_sin[:], in0=u_pairs[:, :, :, ::-1], in1=signed_sin[:])
-        k_chunk = new_chunk()
-        half_regroup(on_vector, k_chunk, w_k_raw[0], 0)
         rotary = keep.tile([P, S_TILES, D_HR], F32)
         nc.vector.tensor_add(out=rotary[:].rearrange("p j (i e) -> p j i e", e=2), in0=by_cos[:], in1=by_sin[:])
-        half_regroup(on_vector, k_chunk, w_k_raw[0], 1)
 
         k_tiles = []
+        half_heads = GROUP_HEADS // 2
+        rotary_of_half = rotary[:].unsqueeze(1).to_broadcast([P, half_heads, S_TILES, D_HR])
 
         def new_k_tile():
-            k_tile = keep.tile([P, GROUP_HEADS, S_TILES, D_H + D_HR], F32, name="k_tile%d" % len(k_tiles))
-            half = GROUP_HEADS // 2
-            source = rotary[:].unsqueeze(1).to_broadcast([P, half, S_TILES, D_HR])
-            nc.vector.tensor_copy(out=k_tile[:, 0:half, :, D_H:], in_=source)
-            nc.scalar.copy(out=k_tile[:, half:, :, D_H:], in_=source)
-            k_tiles.append(k_tile)
+            k_tiles.append(
+                keep.tile([P, GROUP_HEADS, S_TILES, D_H + D_HR], F32, name="k_tile%d" % len(k_tiles))
+            )
+
+        def fill_k_tile(k_tile):
+            nc.vector.tensor_copy(out=k_tile[:, 0:half_heads, :, D_H:], in_=rotary_of_half)
+            nc.scalar.copy(out=k_tile[:, half_heads:, :, D_H:], in_=rotary_of_half)
 
         new_k_tile()
-        k_q = quantise_chunk("w_k0", k_chunk)
-        for c in range(GROUPS):
+        for j in range(S_TILES):
+            product(j, k_q, k_tiles[0], on_vector if j == S_TILES - 1 else on_scalar)
+        fill_k_tile(k_tiles[0])
+        store(k_tiles[0], k_rows[:, group(0), :])
+        k_chunk = regrouped(on_vector, w_k_raw[1])
+        for c in range(1, GROUPS):
+            k_q = quantise_chunk("w_k%d" % c, k_chunk)
+            if c < K_TILES:
+                new_k_tile()
+                fill_k_tile(k_tiles[c])
             if c + 1 < GROUPS:
                 k_chunk = regrouped(on_vector, w_k_raw[c + 1])
             heads(k_q, k_tiles[c % K_TILES], k_rows[:, group(c), :], [on_scalar, on_vector])
-            if c + 1 < K_TILES:
-                new_k_tile()
-            if c + 1 < GROUPS:
-                k_q = quantise_chunk("w_k%d" % (c + 1), k_chunk)

@@ -69,8 +69,8 @@ def tile_mla_pb_kernel(tc, h, w_ckv, w_k, w_kr, w_v, out_0, out_1):
         def load_w_ckv(g):
             raw = keep.tile([P, PACK, D_CKV], BF16, name="w_ckv_raw%d" % g)
             nc.sync.dma_start(
-                out=raw[:].rearrange("q (u e) c -> q u (e c)", e=2),
-                in_=w_ckv[g * K_PASS : (g + 1) * K_PASS, :].rearrange("(u q e) c -> q u (e c)", u=2, e=2),
+                out=raw[:].rearrange("q t c -> q (t c)"),
+                in_=w_ckv[g * K_PASS : (g + 1) * K_PASS, :].rearrange("(q t) c -> q (t c)", t=PACK),
             )
             w_ckv_raw.append(raw[:])
 
@@ -92,8 +92,8 @@ def tile_mla_pb_kernel(tc, h, w_ckv, w_k, w_kr, w_v, out_0, out_1):
         w_v_raw = load_heads("w_v", w_v, 0, 2)
         w_kr_raw = keep.tile([P, PASSES, PACK, D_HR], BF16)
         nc.sync.dma_start(
-            out=w_kr_raw[:].rearrange("q g (u e) c -> q (g u) (e c)", e=2),
-            in_=w_kr.rearrange("(g u q e) c -> q (g u) (e c)", g=PASSES, u=2, e=2),
+            out=w_kr_raw[:].rearrange("q g t c -> q g (t c)"),
+            in_=w_kr.rearrange("(g q t) c -> q g (t c)", g=PASSES, t=PACK),
         )
         w_v_raw = w_v_raw + load_heads("w_v", w_v, 2, 2)
         w_k_raw = load_heads("w_k", w_k, 0, GROUPS)
@@ -188,7 +188,8 @@ def tile_mla_pb_kernel(tc, h, w_ckv, w_k, w_kr, w_v, out_0, out_1):
                 flipped = banks.tile([P, 2, 2, P], F32, tag="bank")
                 for g in range(2):
                     for u in range(2):
-                        nc.tensor.transpose(flipped[:, g, u, :], h_words[:, block(4 * half + 2 * g + u)], identity[:])
+                        pass_words = h_words[:, (2 * half + g) * 2 * P : (2 * half + g + 1) * 2 * P]
+                        nc.tensor.transpose(flipped[:, g, u, :], pass_words[:, u : 2 * P : 2], identity[:])
                 nc.scalar.copy(
                     out=grouped_words[:, 2 * half : 2 * half + 2], in_=flipped[:].rearrange("q g u s -> q g s u")
                 )
@@ -251,8 +252,8 @@ def tile_mla_pb_kernel(tc, h, w_ckv, w_k, w_kr, w_v, out_0, out_1):
         w_ckv_q.append(quantise_chunk("w_ckv1", w1))
         w_ckv_q.append(quantise_chunk("w_ckv2", w2))
         w_ckv_q.append(quantise_chunk("w_ckv3", w3))
-        h_g2 = transpose_h(2)
         warm(0)
+        h_g2 = transpose_h(2)
         quantise_h(h_g1)
         round_turns()
         c_g0 = latent(0, on_scalar)

@@ -252,28 +252,30 @@ def tile_mla_pb_kernel(tc, h, w_ckv, w_k, w_kr, w_v, out_0, out_1):
         w_ckv_q.append(quantise_chunk("w_ckv1", w1))
         w_ckv_q.append(quantise_chunk("w_ckv2", w2))
         w_ckv_q.append(quantise_chunk("w_ckv3", w3))
-        warm(0)
         h_g2 = transpose_h(2)
+        warm(0)
+        h_g3 = transpose_h(3)
         quantise_h(h_g1)
         round_turns()
-        c_g0 = latent(0, on_scalar)
-        h_g3 = transpose_h(3)
         quantise_h(h_g2)
         part_turns()
-        quantise_c(c_g0)
-        c_g1 = latent(1, on_scalar)
+        c_g0 = latent(0, on_scalar)
+        quantise_h(h_g3)
         sines()
-        cosines()
         v0 = new_chunk()
         half_regroup(on_vector, v0, w_v_raw[0], 0)
-        quantise_h(h_g3)
+        c_g1 = latent(1, on_scalar)
+        cosines()
+        quantise_c(c_g0)
         half_regroup(on_vector, v0, w_v_raw[0], 1)
         c_g2 = latent(2, on_scalar)
         quantise_c(c_g1)
         v_q = [quantise_chunk("w_v0", v0)]
-        c_g3 = latent(3, on_scalar)
+        v1 = new_chunk()
+        half_regroup(on_vector, v1, w_v_raw[1], 0)
         quantise_c(c_g2)
-        v1 = regrouped(on_vector, w_v_raw[1])
+        half_regroup(on_vector, v1, w_v_raw[1], 1)
+        c_g3 = latent(3, on_scalar)
         quantise_c(c_g3)
 
         v_rows = out_1.rearrange("b n (p j) d -> p (b n) (j d)", j=S_TILES)

@@ -24,8 +24,6 @@ N_H = 16
 D_H = 128
 D_HR = 128
 PAIRS = D_HR // 2
-PAIR_BITS = 6
-assert 2**PAIR_BITS == PAIRS
 ROPE_BASE = 10000.0
 
 S_TILES = S // P
@@ -84,11 +82,10 @@ def tile_mla_pb_kernel(tc, h, w_ckv, w_k, w_kr, w_v, out_0, out_1):
             return [raw[:, :, c * GROUP_COLS : (c + 1) * GROUP_COLS] for c in range(groups)]
 
         load_h(0)
-        for g in range(PASSES):
+        load_w_ckv(0)
+        for g in range(1, PASSES):
             load_w_ckv(g)
-        load_h(1)
-        load_h(2)
-        load_h(3)
+            load_h(g)
         w_v_raw = load_heads("w_v", w_v, 0, 2)
         w_kr_raw = keep.tile([P, PASSES, PACK, D_HR], BF16)
         nc.sync.dma_start(
@@ -105,17 +102,19 @@ def tile_mla_pb_kernel(tc, h, w_ckv, w_k, w_kr, w_v, out_0, out_1):
         first_sine = keep.tile([P, 1], F32)
         nc.vector.memset(first_sine[:], 0.0)
         nc.scalar.activation(out=first_sine[:], in_=first_sine[:], func=ACT.Sin)
-        position_turns = keep.tile([P, S_TILES], F32)
-        nc.vector.tensor_scalar_mul(out=position_turns[:], in0=position[:], scalar1=1.0 / (2.0 * math.pi))
         frequency = keep.tile([P, PAIRS], F32)
         nc.vector.memset(frequency[:, 0:1], 1.0)
-        for step in range(PAIR_BITS):
-            width = 2**step
-            nc.vector.tensor_scalar_mul(
-                out=frequency[:, width : 2 * width],
-                in0=frequency[:, 0:width],
-                scalar1=ROPE_BASE ** (-2.0 * width / D_HR),
-            )
+        width = 1
+        while width < PAIRS:
+            for copy_index in range(1, 4):
+                nc.vector.tensor_scalar_mul(
+                    out=frequency[:, copy_index * width : (copy_index + 1) * width],
+                    in0=frequency[:, 0:width],
+                    scalar1=ROPE_BASE ** (-2.0 * copy_index * width / D_HR),
+                )
+            width = 4 * width
+        position_turns = keep.tile([P, S_TILES], F32)
+        nc.vector.tensor_scalar_mul(out=position_turns[:], in0=position[:], scalar1=1.0 / (2.0 * math.pi))
         table_shape = [P, S_TILES, PAIRS]
         phase = keep.tile([P, 2, S_TILES, PAIRS], F32)
         nc.vector.tensor_mul(
@@ -129,13 +128,10 @@ def tile_mla_pb_kernel(tc, h, w_ckv, w_k, w_kr, w_v, out_0, out_1):
         signed_sin = keep.tile([P, S_TILES, PAIRS, 2], F32)
         cosine = keep.tile([P, S_TILES, PAIRS], F32)
 
-        def round_turns():
-            nc.vector.tensor_scalar(
-                out=whole[:], in0=phase[:], scalar1=ROUND, scalar2=ROUND, op0=ALU.add, op1=ALU.subtract
-            )
-
-        def part_turns():
-            nc.vector.tensor_sub(out=part_turn[:], in0=phase[:], in1=whole[:])
+        nc.vector.tensor_scalar(
+            out=whole[:], in0=phase[:], scalar1=ROUND, scalar2=ROUND, op0=ALU.add, op1=ALU.subtract
+        )
+        nc.vector.tensor_sub(out=part_turn[:], in0=phase[:], in1=whole[:])
 
         def sines():
             for e in range(2):
@@ -225,7 +221,7 @@ def tile_mla_pb_kernel(tc, h, w_ckv, w_k, w_kr, w_v, out_0, out_1):
             copy(out=out_tile[:, :, j, 0:D_H], in_=bank[:])
 
         def store(out_tile, out_rows):
-            nc.sync.dma_start(out=out_rows, in_=out_tile[:].rearrange("p n j d -> p n (j d)"))
+            nc.sync.dma_start(out=out_rows, in_=out_tile.rearrange("p n j d -> p n (j d)"))
 
         def group(c):
             return slice(c * GROUP_HEADS, (c + 1) * GROUP_HEADS)
@@ -233,50 +229,59 @@ def tile_mla_pb_kernel(tc, h, w_ckv, w_k, w_kr, w_v, out_0, out_1):
         on_vector = nc.vector.tensor_copy
         on_scalar = nc.scalar.copy
 
-        def half_regroup(copy, chunk, raw, half):
-            cols = slice(half * GROUP_COLS // 2, (half + 1) * GROUP_COLS // 2)
+        def part_regroup(copy, chunk, raw, first, end):
+            cols = slice(first * GROUP_COLS // 8, end * GROUP_COLS // 8)
             regroup(copy, chunk[:, cols], raw[:, :, cols])
 
+        def half_regroup(copy, chunk, raw, half):
+            part_regroup(copy, chunk, raw, 4 * half, 4 * half + 4)
+
         h_g0 = transpose_h(0)
-        for g in range(PASSES):
-            warm(g)
+        warm(1)
         w0 = regrouped(on_vector, w_ckv_raw[0])
         quantise_h(h_g0)
         w1 = regrouped(on_scalar, w_ckv_raw[1])
         w_ckv_q = [quantise_chunk("w_ckv0", w0)]
-        w2 = regrouped(on_vector, w_ckv_raw[2])
-        w3 = new_chunk()
-        half_regroup(on_vector, w3, w_ckv_raw[3], 0)
-        half_regroup(on_scalar, w3, w_ckv_raw[3], 1)
         h_g1 = transpose_h(1)
+        warm(2)
+        w2 = regrouped(on_vector, w_ckv_raw[2])
         w_ckv_q.append(quantise_chunk("w_ckv1", w1))
         w_ckv_q.append(quantise_chunk("w_ckv2", w2))
-        w_ckv_q.append(quantise_chunk("w_ckv3", w3))
+        w3 = new_chunk()
+        part_regroup(on_vector, w3, w_ckv_raw[3], 0, 5)
+        part_regroup(on_scalar, w3, w_ckv_raw[3], 5, 8)
         h_g2 = transpose_h(2)
-        warm(0)
+        warm(3)
+        w_ckv_q.append(quantise_chunk("w_ckv3", w3))
         h_g3 = transpose_h(3)
         quantise_h(h_g1)
-        round_turns()
-        quantise_h(h_g2)
-        part_turns()
-        c_g0 = latent(0, on_scalar)
-        quantise_h(h_g3)
         sines()
+        cosines()
+        c_g0 = latent(0, on_scalar)
+        quantise_h(h_g2)
         v0 = new_chunk()
         half_regroup(on_vector, v0, w_v_raw[0], 0)
-        c_g1 = latent(1, on_scalar)
-        cosines()
-        quantise_c(c_g0)
+        quantise_h(h_g3)
         half_regroup(on_vector, v0, w_v_raw[0], 1)
-        c_g2 = latent(2, on_scalar)
-        quantise_c(c_g1)
-        v_q = [quantise_chunk("w_v0", v0)]
+        quantise_c(c_g0)
         v1 = new_chunk()
         half_regroup(on_vector, v1, w_v_raw[1], 0)
-        quantise_c(c_g2)
+        c_g1 = latent(1, on_scalar)
+        v_q = [quantise_chunk("w_v0", v0)]
+        quantise_c(c_g1)
         half_regroup(on_vector, v1, w_v_raw[1], 1)
+        c_g2 = latent(2, on_scalar)
         c_g3 = latent(3, on_scalar)
+        quantise_c(c_g2)
+        kr_grouped = keep.tile([P, PASSES, D_HR, PACK], BF16, align_bytes=64)
+
+        def half_regroup_kr(half):
+            passes = slice(half * PASSES // 2, (half + 1) * PASSES // 2)
+            nc.vector.tensor_copy(out=kr_grouped[:, passes], in_=w_kr_raw[:, passes].rearrange("p g t c -> p g c t"))
+
+        v1_q = quantise_chunk("w_v1", v1)
         quantise_c(c_g3)
+        half_regroup_kr(0)
 
         v_rows = out_1.rearrange("b n (p j) d -> p (b n) (j d)", j=S_TILES)
         k_rows = out_0.rearrange("b n (p j) d -> p (b n) (j d)", j=S_TILES)
@@ -284,43 +289,39 @@ def tile_mla_pb_kernel(tc, h, w_ckv, w_k, w_kr, w_v, out_0, out_1):
         def heads(w_q, out_tile, out_rows, copies):
             for j in range(S_TILES):
                 product(j, w_q, out_tile, copies[j % len(copies)])
-            store(out_tile, out_rows)
+            store(out_tile[:], out_rows)
 
         def new_v_tile(c):
             return v_pool.tile([P, GROUP_HEADS, S_TILES, D_H], F32, tag="v_tile", name="v_tile%d" % c)
 
         heads(v_q[0], new_v_tile(0), v_rows[:, group(0), :], [on_scalar])
-        v_q.append(quantise_chunk("w_v1", v1))
+        v_q.append(v1_q)
         heads(v_q[1], new_v_tile(1), v_rows[:, group(1), :], [on_scalar])
-
-        kr_grouped = keep.tile([P, PASSES, D_HR, PACK], BF16, align_bytes=64)
-
-        def half_regroup_kr(half):
-            passes = slice(half * PASSES // 2, (half + 1) * PASSES // 2)
-            nc.vector.tensor_copy(out=kr_grouped[:, passes], in_=w_kr_raw[:, passes].rearrange("p g t c -> p g c t"))
-
         v2 = regrouped(on_vector, w_v_raw[2])
-        half_regroup_kr(0)
-        v_q.append(quantise_chunk("w_v2", v2))
-        heads(v_q[2], new_v_tile(2), v_rows[:, group(2), :], [on_scalar])
-        v3 = regrouped(on_vector, w_v_raw[3])
         half_regroup_kr(1)
-        v_q.append(quantise_chunk("w_v3", v3))
+        v_q.append(quantise_chunk("w_v2", v2))
         w_kr_q = quantise("w_kr", kr_grouped[:].rearrange("p g c t -> p (g c t)"))
-        heads(v_q[3], new_v_tile(3), v_rows[:, group(3), :], [on_scalar])
+        heads(v_q[2], new_v_tile(2), v_rows[:, group(2), :], [on_scalar])
         u_sum = u_bank.tile([P, S_TILES, D_HR], F32, tag="u")
         for j in range(S_TILES):
             for g in range(PASSES):
                 mx(u_sum[:, j, :], h_q[j], block(g), w_kr_q, block(g), g == 0, g == PASSES - 1)
+        v3 = regrouped(on_vector, w_v_raw[3])
+        v_q.append(quantise_chunk("w_v3", v3))
+        k_chunk = new_chunk()
+        half_regroup(on_vector, k_chunk, w_k_raw[0], 0)
+        heads(v_q[3], new_v_tile(3), v_rows[:, group(3), :], [on_scalar])
 
         pair_shape = [P, S_TILES, PAIRS, 2]
         u_pairs = u_sum[:].rearrange("p j (i e) -> p j i e", e=2)
-        k_chunk = regrouped(on_vector, w_k_raw[0])
-        k_q = quantise_chunk("w_k0", k_chunk)
+        half_regroup(on_vector, k_chunk, w_k_raw[0], 1)
         by_cos = keep.tile(pair_shape, F32)
         nc.vector.tensor_mul(out=by_cos[:], in0=u_pairs, in1=cosine[:].unsqueeze(3).to_broadcast(pair_shape))
+        k_q = quantise_chunk("w_k0", k_chunk)
         by_sin = keep.tile(pair_shape, F32)
         nc.vector.tensor_mul(out=by_sin[:], in0=u_pairs[:, :, :, ::-1], in1=signed_sin[:])
+        next_chunk = new_chunk()
+        half_regroup(on_vector, next_chunk, w_k_raw[1], 0)
         rotary = keep.tile([P, S_TILES, D_HR], F32)
         nc.vector.tensor_add(out=rotary[:].rearrange("p j (i e) -> p j i e", e=2), in0=by_cos[:], in1=by_sin[:])
 
@@ -341,8 +342,9 @@ def tile_mla_pb_kernel(tc, h, w_ckv, w_k, w_kr, w_v, out_0, out_1):
         for j in range(S_TILES):
             product(j, k_q, k_tiles[0], on_vector if j == S_TILES - 1 else on_scalar)
         fill_k_tile(k_tiles[0])
-        store(k_tiles[0], k_rows[:, group(0), :])
-        k_chunk = regrouped(on_vector, w_k_raw[1])
+        store(k_tiles[0][:], k_rows[:, group(0), :])
+        half_regroup(on_vector, next_chunk, w_k_raw[1], 1)
+        k_chunk = next_chunk
         for c in range(1, GROUPS):
             k_q = quantise_chunk("w_k%d" % c, k_chunk)
             if c < K_TILES:

@@ -259,29 +259,30 @@ def tile_mla_pb_kernel(tc, h, w_ckv, w_k, w_kr, w_v, out_0, out_1):
         cosines()
         c_g0 = latent(0, on_scalar)
         quantise_h(h_g2)
+        kr_grouped = keep.tile([P, PASSES, D_HR, PACK], BF16, align_bytes=64)
+
+        def regroup_kr(copy, first, end):
+            copy(out=kr_grouped[:, first:end], in_=w_kr_raw[:, first:end].rearrange("p g t c -> p g c t"))
+
         v0 = new_chunk()
         half_regroup(on_vector, v0, w_v_raw[0], 0)
         quantise_h(h_g3)
         half_regroup(on_vector, v0, w_v_raw[0], 1)
         quantise_c(c_g0)
         v1 = new_chunk()
-        half_regroup(on_vector, v1, w_v_raw[1], 0)
+        part_regroup(on_vector, v1, w_v_raw[1], 0, 4)
+        part_regroup(on_scalar, v1, w_v_raw[1], 6, 8)
         c_g1 = latent(1, on_scalar)
         v_q = [quantise_chunk("w_v0", v0)]
         quantise_c(c_g1)
-        half_regroup(on_vector, v1, w_v_raw[1], 1)
+        part_regroup(on_vector, v1, w_v_raw[1], 4, 6)
         c_g2 = latent(2, on_scalar)
+        regroup_kr(on_scalar, 3, 4)
         c_g3 = latent(3, on_scalar)
         quantise_c(c_g2)
-        kr_grouped = keep.tile([P, PASSES, D_HR, PACK], BF16, align_bytes=64)
-
-        def half_regroup_kr(half):
-            passes = slice(half * PASSES // 2, (half + 1) * PASSES // 2)
-            nc.vector.tensor_copy(out=kr_grouped[:, passes], in_=w_kr_raw[:, passes].rearrange("p g t c -> p g c t"))
-
         v1_q = quantise_chunk("w_v1", v1)
         quantise_c(c_g3)
-        half_regroup_kr(0)
+        regroup_kr(on_vector, 0, 2)
 
         v_rows = out_1.rearrange("b n (p j) d -> p (b n) (j d)", j=S_TILES)
         k_rows = out_0.rearrange("b n (p j) d -> p (b n) (j d)", j=S_TILES)
@@ -298,7 +299,7 @@ def tile_mla_pb_kernel(tc, h, w_ckv, w_k, w_kr, w_v, out_0, out_1):
         v_q.append(v1_q)
         heads(v_q[1], new_v_tile(1), v_rows[:, group(1), :], [on_scalar])
         v2 = regrouped(on_vector, w_v_raw[2])
-        half_regroup_kr(1)
+        regroup_kr(on_vector, 2, 3)
         v_q.append(quantise_chunk("w_v2", v2))
         w_kr_q = quantise("w_kr", kr_grouped[:].rearrange("p g c t -> p (g c t)"))
         heads(v_q[2], new_v_tile(2), v_rows[:, group(2), :], [on_scalar])

import math
from contextlib import ExitStack

import concourse.mybir as mybir
from concourse.masks import make_identity

F32 = mybir.dt.float32
BF16 = mybir.dt.bfloat16
I32 = mybir.dt.int32
U32 = mybir.dt.uint32
U8 = mybir.dt.uint8
FP8X4 = mybir.dt.float8_e4m3fn_x4
ALU = mybir.AluOpType
ACT = mybir.ActivationFunctionType

P = 128
PACK = 4
K_PASS = P * PACK

S = 512
D_MODEL = 2048
D_CKV = 512
N_H = 16
D_H = 128
D_HR = 128
PAIRS = D_HR // 2
ROPE_BASE = 10000.0

S_TILES = S // P
PASSES = D_MODEL // K_PASS
CKV_TILES = D_CKV // P
GROUP_HEADS = 4
GROUP_COLS = GROUP_HEADS * D_H
GROUPS = N_H // GROUP_HEADS
K_TILES = 3
ROUND = 1.5 * 2.0**23

FLOPS = 2 * S * (D_MODEL * D_CKV + D_MODEL * D_HR + 2 * D_CKV * N_H * D_H)


def tile_mla_pb_kernel(tc, h, w_ckv, w_k, w_kr, w_v, out_0, out_1):
    nc = tc.nc
    with ExitStack() as ctx:
        keep = ctx.enter_context(tc.tile_pool(name="keep", bufs=1))
        grouped_pool = ctx.enter_context(tc.tile_pool(name="grouped", bufs=4))
        h_pool = ctx.enter_context(tc.tile_pool(name="h_grouped", bufs=3))
        v_pool = ctx.enter_context(tc.tile_pool(name="v_tiles", bufs=3))
        banks = ctx.enter_context(tc.psum_pool(name="banks", bufs=7))
        u_bank = ctx.enter_context(tc.psum_pool(name="u_bank", bufs=1))
        ctx.enter_context(tc.manual_schedule())

        def block(i):
            return slice(i * P, (i + 1) * P)

        everything = slice(None)

        h_rows = h.rearrange("b (p j) k -> p (b j) k", j=S_TILES)
        h_raw = []

        def load_h(j):
            raw = keep.tile([P, D_MODEL], BF16, name="h_raw%d" % j)
            nc.sync.dma_start(out=raw[:], in_=h_rows[:, j, :])
            h_raw.append(raw)

        w_ckv_raw = []

        def load_w_ckv(g):
            raw = keep.tile([P, PACK, D_CKV], BF16, name="w_ckv_raw%d" % g)
            nc.sync.dma_start(
                out=raw[:].rearrange("q t c -> q (t c)"),
                in_=w_ckv[g * K_PASS : (g + 1) * K_PASS, :].rearrange("(q t) c -> q (t c)", t=PACK),
            )
            w_ckv_raw.append(raw[:])

        def load_heads(name, w, first_group, groups):
            raw = keep.tile([P, PACK, groups * GROUP_COLS], BF16, name="%s_raw%d" % (name, first_group))
            first = first_group * GROUP_COLS
            nc.sync.dma_start(
                out=raw[:],
                in_=w.rearrange("(t p) n -> p t n", t=PACK)[:, :, first : first + groups * GROUP_COLS],
            )
            return [raw[:, :, c * GROUP_COLS : (c + 1) * GROUP_COLS] for c in range(groups)]

        load_h(0)
        load_w_ckv(0)
        for g in range(1, PASSES):
            load_w_ckv(g)
            load_h(g)
        w_v_raw = load_heads("w_v", w_v, 0, 2)
        w_kr_raw = keep.tile([P, PASSES, PACK, D_HR], BF16)
        nc.sync.dma_start(
            out=w_kr_raw[:].rearrange("q g t c -> q g (t c)"),
            in_=w_kr.rearrange("(g q t) c -> q g (t c)", g=PASSES, t=PACK),
        )
        w_v_raw = w_v_raw + load_heads("w_v", w_v, 2, 2)
        w_k_raw = load_heads("w_k", w_k, 0, GROUPS)

        identity = keep.tile([P, P], F32)
        make_identity(nc, identity[:])
        position = keep.tile([P, S_TILES], I32)
        nc.gpsimd.iota(position[:], pattern=[[1, S_TILES]], base=0, channel_multiplier=S_TILES)
        first_sine = keep.tile([P, 1], F32)
        nc.vector.memset(first_sine[:], 0.0)
        nc.scalar.activation(out=first_sine[:], in_=first_sine[:], func=ACT.Sin)
        frequency = keep.tile([P, PAIRS], F32)
        nc.vector.memset(frequency[:, 0:1], 1.0)
        width = 1
        while width < PAIRS:
            for copy_index in range(1, 4):
                nc.vector.tensor_scalar_mul(
                    out=frequency[:, copy_index * width : (copy_index + 1) * width],
                    in0=frequency[:, 0:width],
                    scalar1=ROPE_BASE ** (-2.0 * copy_index * width / D_HR),
                )
            width = 4 * width
        position_turns = keep.tile([P, S_TILES], F32)
        nc.vector.tensor_scalar_mul(out=position_turns[:], in0=position[:], scalar1=1.0 / (2.0 * math.pi))
        table_shape = [P, S_TILES, PAIRS]
        phase = keep.tile([P, 2, S_TILES, PAIRS], F32)
        nc.vector.tensor_mul(
            out=phase[:, 0],
            in0=frequency[:].unsqueeze(1).to_broadcast(table_shape),
            in1=position_turns[:].unsqueeze(2).to_broadcast(table_shape),
        )
        nc.vector.tensor_scalar_add(out=phase[:, 1], in0=phase[:, 0], scalar1=0.25)
        whole = keep.tile([P, 2, S_TILES, PAIRS], F32)
        part_turn = keep.tile([P, 2, S_TILES, PAIRS], F32)
        signed_sin = keep.tile([P, S_TILES, PAIRS, 2], F32)
        cosine = keep.tile([P, S_TILES, PAIRS], F32)

        nc.vector.tensor_scalar(
            out=whole[:], in0=phase[:], scalar1=ROUND, scalar2=ROUND, op0=ALU.add, op1=ALU.subtract
        )
        nc.vector.tensor_sub(out=part_turn[:], in0=phase[:], in1=whole[:])

        def sines():
            for e in range(2):
                scale = (2 * e - 1) * 2.0 * math.pi
                nc.scalar.activation(out=signed_sin[:, :, :, e], in_=part_turn[:, 0], func=ACT.Sin, scale=scale)

        def cosines():
            nc.scalar.activation(out=cosine[:], in_=part_turn[:, 1], func=ACT.Sin, scale=2.0 * math.pi)

        def regroup(copy, grouped, raw):
            copy(
                out=grouped.rearrange("p (c i) t -> p c t i", i=4),
                in_=raw.rearrange("p t (c i) -> p c t i", i=4),
            )

        def new_chunk():
            return grouped_pool.tile([P, GROUP_COLS, PACK], BF16, tag="grouped", name="chunk", align_bytes=64)

        def regrouped(copy, raw):
            chunk = new_chunk()
            regroup(copy, chunk[:], raw)
            return chunk

        def quantise(name, grouped_flat):
            words = grouped_flat.shape[1] // PACK
            codes = keep.tile([P, words], U32, name=name + "_codes", align_bytes=64)
            scales = keep.tile([P, words], U8, name=name + "_scales", align_bytes=64)
            nc.vector.quantize_mx(out=codes[:].bitcast(FP8X4), scales=scales[:], in_=grouped_flat)
            return codes, scales

        def quantise_chunk(name, chunk):
            return quantise(name, chunk[:].rearrange("p c t -> p (c t)"))

        def mx(out, stationary, m_cols, moving, n_cols, start, stop):
            nc.tensor.matmul_mx(
                out=out,
                lhsT=stationary[0][:, m_cols].bitcast(FP8X4),
                lhsT_scale=stationary[1][:, m_cols],
                rhs=moving[0][:, n_cols].bitcast(FP8X4),
                rhs_scale=moving[1][:, n_cols],
                start=start,
                stop=stop,
            )

        def transpose_h(j):
            h_words = h_raw[j][:].bitcast(F32)
            h_grouped = h_pool.tile([P, D_MODEL], BF16, tag="h_grouped", align_bytes=64)
            grouped_words = h_grouped[:].bitcast(F32).rearrange("q (g s u) -> q g s u", g=PASSES, u=2)
            for half in range(2):
                flipped = banks.tile([P, 2, 2, P], F32, tag="bank")
                for g in range(2):
                    for u in range(2):
                        pass_words = h_words[:, (2 * half + g) * 2 * P : (2 * half + g + 1) * 2 * P]
                        nc.tensor.transpose(flipped[:, g, u, :], pass_words[:, u : 2 * P : 2], identity[:])
                nc.scalar.copy(
                    out=grouped_words[:, 2 * half : 2 * half + 2], in_=flipped[:].rearrange("q g u s -> q g s u")
                )
            return h_grouped

        def warm(g):
            bank = u_bank.tile([P, D_CKV], F32, tag="u")
            for t in range(2):
                nc.tensor.matmul(bank[:], w_ckv_raw[g][:, t, 0:P], w_ckv_raw[g][:, t + 2, :], start=True, stop=True)

        h_q = []

        def quantise_h(h_grouped):
            h_q.append(quantise("h%d" % len(h_q), h_grouped[:]))

        def latent(j, copy):
            c_kv = banks.tile([P, CKV_TILES, P], F32, tag="bank")
            for t in range(CKV_TILES):
                for g in range(PASSES):
                    mx(c_kv[:, t, :], w_ckv_q[g], block(t), h_q[j], block(g), g == 0, g == PASSES - 1)
            c_grouped = h_pool.tile([P, P, PACK], BF16, tag="c_grouped", align_bytes=64)
            copy(out=c_grouped[:], in_=c_kv[:].rearrange("p t s -> p s t"))
            return c_grouped

        c_q = []

        def quantise_c(c_grouped):
            c_q.append(quantise("c_kv%d" % len(c_q), c_grouped[:].rearrange("p s t -> p (s t)")))

        def product(j, w_q, out_tile, copy):
            bank = banks.tile([P, GROUP_HEADS, D_H], F32, tag="bank")
            mx(bank[:].rearrange("p n d -> p (n d)"), c_q[j], everything, w_q, everything, True, True)
            copy(out=out_tile[:, :, j, 0:D_H], in_=bank[:])

        def store(out_tile, out_rows):
            nc.sync.dma_start(out=out_rows, in_=out_tile.rearrange("p n j d -> p n (j d)"))

        def group(c):
            return slice(c * GROUP_HEADS, (c + 1) * GROUP_HEADS)

        on_vector = nc.vector.tensor_copy
        on_scalar = nc.scalar.copy

        def part_regroup(copy, chunk, raw, first, end):
            cols = slice(first * GROUP_COLS // 8, end * GROUP_COLS // 8)
            regroup(copy, chunk[:, cols], raw[:, :, cols])

        def half_regroup(copy, chunk, raw, half):
            part_regroup(copy, chunk, raw, 4 * half, 4 * half + 4)

        h_g0 = transpose_h(0)
        warm(1)
        w0 = regrouped(on_vector, w_ckv_raw[0])
        quantise_h(h_g0)
        w1 = regrouped(on_scalar, w_ckv_raw[1])
        w_ckv_q = [quantise_chunk("w_ckv0", w0)]
        h_g1 = transpose_h(1)
        warm(2)
        w2 = regrouped(on_vector, w_ckv_raw[2])
        w_ckv_q.append(quantise_chunk("w_ckv1", w1))
        w_ckv_q.append(quantise_chunk("w_ckv2", w2))
        w3 = new_chunk()
        part_regroup(on_vector, w3, w_ckv_raw[3], 0, 5)
        part_regroup(on_scalar, w3, w_ckv_raw[3], 5, 8)
        h_g2 = transpose_h(2)
        warm(3)
        w_ckv_q.append(quantise_chunk("w_ckv3", w3))
        h_g3 = transpose_h(3)
        quantise_h(h_g1)
        sines()
        cosines()
        c_g0 = latent(0, on_scalar)
        quantise_h(h_g2)
        kr_grouped = keep.tile([P, PASSES, D_HR, PACK], BF16, align_bytes=64)

        def regroup_kr(copy, first, end):
            copy(out=kr_grouped[:, first:end], in_=w_kr_raw[:, first:end].rearrange("p g t c -> p g c t"))

        v0 = new_chunk()
        half_regroup(on_vector, v0, w_v_raw[0], 0)
        quantise_h(h_g3)
        half_regroup(on_vector, v0, w_v_raw[0], 1)
        quantise_c(c_g0)
        v1 = new_chunk()
        part_regroup(on_vector, v1, w_v_raw[1], 0, 4)
        part_regroup(on_scalar, v1, w_v_raw[1], 6, 8)
        c_g1 = latent(1, on_scalar)
        v_q = [quantise_chunk("w_v0", v0)]
        quantise_c(c_g1)
        part_regroup(on_vector, v1, w_v_raw[1], 4, 6)
        c_g2 = latent(2, on_scalar)
        regroup_kr(on_scalar, 3, 4)
        c_g3 = latent(3, on_scalar)
        quantise_c(c_g2)
        v1_q = quantise_chunk("w_v1", v1)
        quantise_c(c_g3)
        regroup_kr(on_vector, 0, 2)

        v_rows = out_1.rearrange("b n (p j) d -> p (b n) (j d)", j=S_TILES)
        k_rows = out_0.rearrange("b n (p j) d -> p (b n) (j d)", j=S_TILES)

        def heads(w_q, out_tile, out_rows, copies):
            for j in range(S_TILES):
                product(j, w_q, out_tile, copies[j % len(copies)])
            store(out_tile[:], out_rows)

        def new_v_tile(c):
            return v_pool.tile([P, GROUP_HEADS, S_TILES, D_H], F32, tag="v_tile", name="v_tile%d" % c)

        heads(v_q[0], new_v_tile(0), v_rows[:, group(0), :], [on_scalar])
        v_q.append(v1_q)
        heads(v_q[1], new_v_tile(1), v_rows[:, group(1), :], [on_scalar])
        v2 = regrouped(on_vector, w_v_raw[2])
        regroup_kr(on_vector, 2, 3)
        v_q.append(quantise_chunk("w_v2", v2))
        w_kr_q = quantise("w_kr", kr_grouped[:].rearrange("p g c t -> p (g c t)"))
        heads(v_q[2], new_v_tile(2), v_rows[:, group(2), :], [on_scalar])
        u_sum = u_bank.tile([P, S_TILES, D_HR], F32, tag="u")
        for j in range(S_TILES):
            for g in range(PASSES):
                mx(u_sum[:, j, :], h_q[j], block(g), w_kr_q, block(g), g == 0, g == PASSES - 1)
        v3 = regrouped(on_vector, w_v_raw[3])
        v_q.append(quantise_chunk("w_v3", v3))
        k_chunk = new_chunk()
        half_regroup(on_vector, k_chunk, w_k_raw[0], 0)
        heads(v_q[3], new_v_tile(3), v_rows[:, group(3), :], [on_scalar])

        pair_shape = [P, S_TILES, PAIRS, 2]
        u_pairs = u_sum[:].rearrange("p j (i e) -> p j i e", e=2)
        half_regroup(on_vector, k_chunk, w_k_raw[0], 1)
        by_cos = keep.tile(pair_shape, F32)
        nc.vector.tensor_mul(out=by_cos[:], in0=u_pairs, in1=cosine[:].unsqueeze(3).to_broadcast(pair_shape))
        k_q = quantise_chunk("w_k0", k_chunk)
        by_sin = keep.tile(pair_shape, F32)
        nc.vector.tensor_mul(out=by_sin[:], in0=u_pairs[:, :, :, ::-1], in1=signed_sin[:])
        next_chunk = new_chunk()
        half_regroup(on_vector, next_chunk, w_k_raw[1], 0)
        rotary = keep.tile([P, S_TILES, D_HR], F32)
        nc.vector.tensor_add(out=rotary[:].rearrange("p j (i e) -> p j i e", e=2), in0=by_cos[:], in1=by_sin[:])

        k_tiles = []
        half_heads = GROUP_HEADS // 2
        rotary_of_half = rotary[:].unsqueeze(1).to_broadcast([P, half_heads, S_TILES, D_HR])

        def new_k_tile():
            k_tiles.append(
                keep.tile([P, GROUP_HEADS, S_TILES, D_H + D_HR], F32, name="k_tile%d" % len(k_tiles))
            )

        def fill_k_tile(k_tile):
            nc.vector.tensor_copy(out=k_tile[:, 0:half_heads, :, D_H:], in_=rotary_of_half)
            nc.scalar.copy(out=k_tile[:, half_heads:, :, D_H:], in_=rotary_of_half)

        new_k_tile()
        for j in range(S_TILES):
            product(j, k_q, k_tiles[0], on_vector if j == S_TILES - 1 else on_scalar)
        fill_k_tile(k_tiles[0])
        store(k_tiles[0][:], k_rows[:, group(0), :])
        half_regroup(on_vector, next_chunk, w_k_raw[1], 1)
        k_chunk = next_chunk
        for c in range(1, GROUPS):
            k_q = quantise_chunk("w_k%d" % c, k_chunk)
            if c < K_TILES:
                new_k_tile()
                fill_k_tile(k_tiles[c])
            if c + 1 < GROUPS:
                k_chunk = regrouped(on_vector, w_k_raw[c + 1])
            heads(k_q, k_tiles[c % K_TILES], k_rows[:, group(c), :], [on_scalar, on_vector])
